import numpy as np
import ml_dtypes


def mxq(x, axis, fmt="e4m3"):
    dtype, down = {"e4m3": (ml_dtypes.float8_e4m3fn, 7), "e5m2": (ml_dtypes.float8_e5m2, 14)}[fmt]
    v = np.moveaxis(np.asarray(x, np.float32).astype(ml_dtypes.bfloat16).astype(np.float64), axis, -1)
    blocks = v.reshape(v.shape[:-1] + (-1, 32))
    amax = np.abs(blocks).max(-1, keepdims=True)
    byte = np.maximum(np.where(amax > 0, np.frexp(amax)[1] - 1 + 127, 0) - down, 1)
    scale = np.exp2(byte - 127.0)
    codes = (blocks / scale).astype(np.float32).astype(dtype).astype(np.float64)
    return np.moveaxis((codes * scale).reshape(v.shape), -1, axis)


WIDE = False


def mx_kscale(k):
    if not WIDE:
        return np.ones(k)
    levels = np.array([20, -20, 10, -10, 0])
    a = np.random.permutation(np.resize(levels, k // 512 * 4)).reshape(k // 512, 4)
    idx = np.arange(k)
    return np.exp2(a[idx // 512, idx % 128 // 32])


BF16 = ml_dtypes.bfloat16


def bf(x):
    return np.asarray(x, np.float32).astype(BF16)


def f64(x):
    return np.asarray(x).astype(np.float64)


B, S, HID, NH, NOPE, ROPE, VD, KV_RANK, SW, QB = 1, 1024, 512, 8, 256, 768, 128, 512, 384, 128
QK = NOPE + ROPE


def rotate_half(x):
    h = x.shape[-1] // 2
    return np.concatenate([-x[..., h:], x[..., :h]], axis=-1)


def rotate_half_t(y):
    h = y.shape[-1] // 2
    return np.concatenate([y[..., h:], -y[..., :h]], axis=-1)


def rope_tables():
    pos = np.arange(S, dtype=np.float64)
    inv = 1.0 / (10000.0 ** (np.arange(0, ROPE, 2, dtype=np.float64) / ROPE))
    ang = pos[:, None] * inv[None, :]
    ang = np.concatenate([ang, ang], axis=-1)
    return bf(np.broadcast_to(np.cos(ang)[None], (B, S, ROPE))), bf(np.broadcast_to(np.sin(ang)[None], (B, S, ROPE)))


def setup_inputs():
    u = np.array(mx_kscale(NH * QK), dtype=np.float64).reshape(NH, QK)
    u[:, NOPE + ROPE // 2:] = u[:, NOPE:NOPE + ROPE // 2]
    cos, sin = rope_tables()
    hs = np.random.standard_normal((B, S, HID))
    wq = np.random.standard_normal((HID, NH * QK)) * 2.0 / np.sqrt(HID) / u.reshape(-1)[None, :]
    b = np.random.standard_normal(NH * QK) * 0.2
    g = np.random.standard_normal((B, NH, S, QK)) * np.exp2(np.random.randint(-12, 1, (B, 1, S, 1))) * 4.0 * u[None, :, None, :]
    return {"hidden_states": bf(hs), "cos": cos, "sin": sin, "Wq": bf(wq), "bq": bf(b), "grad_out": bf(g)}


def reference(hidden_states, cos, sin, Wq, bq, grad_out):
    g = f64(grad_out)
    c, si = f64(cos)[:, None], f64(sin)[:, None]
    g_nope, g_rope = g[..., :NOPE], g[..., NOPE:]
    gq_rope = g_rope * c + rotate_half_t(g_rope * si)
    gq = np.concatenate([g_nope, gq_rope], axis=-1).transpose(0, 2, 1, 3).reshape(B, S, NH * QK)
    return mxq(gq, 2, "e5m2") @ mxq(f64(Wq), 1, "e4m3").T

@@ -1,0 +1,236 @@
+from contextlib import ExitStack
+
+import concourse.masks as masks
+import concourse.mybir as mybir
+
+F32 = mybir.dt.float32
+BF16 = mybir.dt.bfloat16
+U32 = mybir.dt.uint32
+U8 = mybir.dt.uint8
+E5M2_X4 = mybir.dt.float8_e5m2_x4
+E4M3_X4 = mybir.dt.float8_e4m3fn_x4
+MULT = mybir.AluOpType.mult
+
+P = 128
+PACK = 4
+K_PASS = P * PACK
+
+TOKENS = 1024
+HIDDEN = 512
+HEADS = 8
+NOPE = 256
+ROPE = 768
+HALF = ROPE // 2
+HEAD_DIM = NOPE + ROPE
+NOPE_ALL = HEADS * NOPE
+ROPE_ALL = HEADS * ROPE
+K_ALL = NOPE_ALL + ROPE_ALL
+
+NOPE_PASSES = NOPE_ALL // K_PASS
+ROPE_PASSES = ROPE_ALL // K_PASS
+PASSES = NOPE_PASSES + ROPE_PASSES
+TOKEN_TILES = TOKENS // P
+HIDDEN_TILES = HIDDEN // P
+
+GROUP_HEADS = 4
+GROUP_PASSES = GROUP_HEADS * ROPE // K_PASS
+GROUP_WORDS = GROUP_HEADS * ROPE // PACK
+HEAD_WORDS = ROPE // PACK
+HALF_WORDS = HALF // PACK
+QUAD = 4
+
+FLOPS = 2 * TOKENS * HIDDEN * K_ALL
+BYTES = 2 * (TOKENS * K_ALL + HIDDEN * K_ALL + 2 * TOKENS * ROPE) + 4 * TOKENS * HIDDEN
+
+
+def load_in_k_order(nc, dest, rows):
+    nc.sync.dma_start(
+        out=dest[:, 0:NOPE_ALL].rearrange("p (h d) -> p h d", h=HEADS),
+        in_=rows[:, :, 0:NOPE],
+    )
+    nc.sync.dma_start(
+        out=dest[:, NOPE_ALL:K_ALL].rearrange("p (h d) -> p h d", h=HEADS),
+        in_=rows[:, :, NOPE:HEAD_DIM],
+    )
+
+
+def words_of_passes(raw, passes):
+    words = raw[:].bitcast(F32)[:, 0 : passes * K_PASS // 2]
+    return words.rearrange("q (c p u) -> q c u p", c=passes, u=2)
+
+
+def tile_gptossmlaattention_pb_k_kernel(
+    tc, hidden_states, cos, sin, Wq, bq, grad_out, out
+):
+    nc = tc.nc
+    with ExitStack() as ctx:
+        keep = ctx.enter_context(tc.tile_pool(name="keep", bufs=1))
+        raw_w = ctx.enter_context(tc.tile_pool(name="raw_w", bufs=2))
+        raw_g = ctx.enter_context(tc.tile_pool(name="raw_g", bufs=3))
+        tables = ctx.enter_context(tc.tile_pool(name="tables", bufs=2))
+        products = ctx.enter_context(tc.tile_pool(name="products", bufs=2))
+        regrouped = ctx.enter_context(tc.tile_pool(name="regrouped", bufs=3))
+        quantised = ctx.enter_context(tc.tile_pool(name="quantised", bufs=2))
+        results = ctx.enter_context(tc.tile_pool(name="results", bufs=2))
+        turned_banks = ctx.enter_context(tc.psum_pool(name="turned_banks", bufs=6))
+        sum_banks = ctx.enter_context(tc.psum_pool(name="sum_banks", bufs=2))
+
+        ident = keep.tile([P, P], F32)
+        masks.make_identity(nc, ident[:])
+        w_codes = keep.tile([P, PASSES * HIDDEN], U32, align_bytes=64)
+        w_scales = keep.tile([P, PASSES * HIDDEN], U8, align_bytes=64)
+
+        def quantise_weights(it):
+            w_raw = raw_w.tile([P, K_ALL], BF16)
+            load_in_k_order(
+                nc, w_raw, Wq[it * P : (it + 1) * P, :].rearrange("i (h d) -> i h d", h=HEADS)
+            )
+            w_words = words_of_passes(w_raw, PASSES)
+            for c0 in range(0, PASSES, 2):
+                turned = turned_banks.tile([P, PACK, P], F32, tag="turned")
+                for cc in range(2):
+                    for u in range(2):
+                        nc.tensor.transpose(
+                            out=turned[:, 2 * cc + u, :],
+                            in_=w_words[:, c0 + cc, u, :],
+                            identity=ident[:],
+                        )
+                w_grouped = regrouped.tile([P, 2 * P * PACK], BF16, align_bytes=64)
+                nc.scalar.copy(
+                    out=w_grouped[:].bitcast(F32).rearrange("p (c i u) -> p c i u", c=2, u=2),
+                    in_=turned[:].rearrange("p (c u) i -> p c i u", u=2),
+                )
+                for cc in range(2):
+                    cols = slice((c0 + cc) * HIDDEN + it * P, (c0 + cc) * HIDDEN + (it + 1) * P)
+                    nc.vector.quantize_mx(
+                        out=w_codes[:, cols].bitcast(E4M3_X4),
+                        scales=w_scales[:, cols],
+                        in_=w_grouped[:, cc * P * PACK : (cc + 1) * P * PACK],
+                    )
+
+        def rope_products(g_raw, cos_t, signed_sin, group):
+            heads = slice(group * GROUP_HEADS, (group + 1) * GROUP_HEADS)
+            rotated = g_raw[:, NOPE_ALL:K_ALL]
+            direct = products.tile([P, PACK, GROUP_WORDS], F32)
+            nc.vector.tensor_tensor(
+                out=direct[:].rearrange("q t (h j) -> q h t j", h=GROUP_HEADS),
+                in0=rotated.rearrange("q (h j t) -> q h t j", h=HEADS, t=PACK)[:, heads],
+                in1=cos_t[:]
+                .rearrange("q (j t) -> q t j", t=PACK)
+                .unsqueeze(1)
+                .to_broadcast([P, GROUP_HEADS, PACK, HEAD_WORDS]),
+                op=MULT,
+            )
+            crossed = products.tile([P, PACK, GROUP_WORDS], F32)
+            for f in range(2):
+                nc.vector.tensor_tensor(
+                    out=crossed[:].rearrange("q t (h f j) -> q f h t j", h=GROUP_HEADS, f=2)[:, f],
+                    in0=rotated.rearrange("q (h f j t) -> q f h t j", h=HEADS, f=2, t=PACK)[
+                        :, 1 - f, heads
+                    ],
+                    in1=signed_sin[:]
+                    .rearrange("q (f j t) -> q f t j", f=2, t=PACK)[:, 1 - f]
+                    .unsqueeze(1)
+                    .to_broadcast([P, GROUP_HEADS, PACK, HALF_WORDS]),
+                    op=MULT,
+                )
+            return direct, crossed
+
+        def quantise_tokens(n):
+            rows = slice(n * P, (n + 1) * P)
+            cos_t = tables.tile([P, ROPE], BF16)
+            nc.sync.dma_start(out=cos_t[:], in_=cos[0, rows, :])
+            signed_sin = tables.tile([P, ROPE], BF16)
+            nc.sync.dma_start(out=signed_sin[:], in_=sin[0, rows, :])
+            g_raw = raw_g.tile([P, K_ALL], BF16)
+            load_in_k_order(nc, g_raw, grad_out[0, :, rows, :].rearrange("h s d -> s h d"))
+            nc.scalar.mul(out=signed_sin[:, 0:HALF], in_=signed_sin[:, 0:HALF], mul=-1.0)
+
+            g_codes = quantised.tile([P, PASSES * P], U32, align_bytes=64)
+            g_scales = quantised.tile([P, PASSES * P], U8, align_bytes=64)
+
+            def quantise_quad(grouped, first_pass):
+                cols = slice(first_pass * P, (first_pass + QUAD) * P)
+                nc.vector.quantize_mx(
+                    out=g_codes[:, cols].bitcast(E5M2_X4),
+                    scales=g_scales[:, cols],
+                    in_=grouped[:],
+                )
+
+            g_words = words_of_passes(g_raw, NOPE_PASSES)
+            grouped = regrouped.tile([P, QUAD * P * PACK], BF16, align_bytes=64)
+            for c0 in range(0, NOPE_PASSES, 2):
+                turned = turned_banks.tile([P, PACK, P], F32, tag="turned")
+                for cc in range(2):
+                    for u in range(2):
+                        nc.tensor.transpose(
+                            out=turned[:, 2 * cc + u, :],
+                            in_=g_words[:, c0 + cc, u, :],
+                            identity=ident[:],
+                        )
+                nc.scalar.copy(
+                    out=grouped[:, c0 * P * PACK : (c0 + 2) * P * PACK]
+                    .bitcast(F32)
+                    .rearrange("p (c r u) -> p c r u", c=2, u=2),
+                    in_=turned[:].rearrange("p (c u) r -> p c r u", u=2),
+                )
+            quantise_quad(grouped, 0)
+
+            for cr in range(ROPE_PASSES):
+                if cr % GROUP_PASSES == 0:
+                    direct, crossed = rope_products(g_raw, cos_t, signed_sin, cr // GROUP_PASSES)
+                if cr % QUAD == 0:
+                    grouped = regrouped.tile([P, QUAD * P * PACK], BF16, align_bytes=64)
+                block = slice((cr % GROUP_PASSES) * P, (cr % GROUP_PASSES + 1) * P)
+                turned = turned_banks.tile([P, PACK, P], F32, tag="turned")
+                for t in range(PACK):
+                    nc.tensor.matmul(
+                        out=turned[:, t, :],
+                        lhsT=direct[:, t, block],
+                        rhs=ident[:],
+                        is_transpose=True,
+                        start=True,
+                        stop=False,
+                    )
+                    nc.tensor.matmul(
+                        out=turned[:, t, :],
+                        lhsT=crossed[:, t, block],
+                        rhs=ident[:],
+                        is_transpose=True,
+                        start=False,
+                        stop=True,
+                    )
+                nc.scalar.copy(
+                    out=grouped[:, (cr % QUAD) * P * PACK : (cr % QUAD + 1) * P * PACK].rearrange(
+                        "p (r t) -> p r t", t=PACK
+                    ),
+                    in_=turned[:].rearrange("p t r -> p r t"),
+                )
+                if cr % QUAD == QUAD - 1:
+                    quantise_quad(grouped, NOPE_PASSES + cr - (QUAD - 1))
+            return g_codes, g_scales
+
+        def multiply(n, g_codes, g_scales):
+            sums = sum_banks.tile([P, HIDDEN], F32)
+            for c in range(PASSES):
+                nc.tensor.matmul_mx(
+                    out=sums[:],
+                    lhsT=g_codes[:, c * P : (c + 1) * P].bitcast(E5M2_X4),
+                    lhsT_scale=g_scales[:, c * P : (c + 1) * P],
+                    rhs=w_codes[:, c * HIDDEN : (c + 1) * HIDDEN].bitcast(E4M3_X4),
+                    rhs_scale=w_scales[:, c * HIDDEN : (c + 1) * HIDDEN],
+                    start=(c == 0),
+                    stop=(c == PASSES - 1),
+                )
+            result = results.tile([P, HIDDEN], F32)
+            nc.scalar.copy(out=result[:], in_=sums[:])
+            nc.sync.dma_start(out=out[0, n * P : (n + 1) * P, :], in_=result[:])
+
+        ready = quantise_tokens(0)
+        for it in range(HIDDEN_TILES):
+            quantise_weights(it)
+        for n in range(1, TOKEN_TILES):
+            following = quantise_tokens(n)
+            multiply(n - 1, ready[0], ready[1])
+            ready = following
+        multiply(TOKEN_TILES - 1, ready[0], ready[1])

@@ -22,41 +22,33 @@ NOPE = 256
 ROPE = 768
 HALF = ROPE // 2
 HEAD_DIM = NOPE + ROPE
-NOPE_ALL = HEADS * NOPE
-ROPE_ALL = HEADS * ROPE
-K_ALL = NOPE_ALL + ROPE_ALL
-
-NOPE_PASSES = NOPE_ALL // K_PASS
-ROPE_PASSES = ROPE_ALL // K_PASS
-PASSES = NOPE_PASSES + ROPE_PASSES
+K_ALL = HEADS * HEAD_DIM
 TOKEN_TILES = TOKENS // P
 HIDDEN_TILES = HIDDEN // P
 
-GROUP_HEADS = 4
-GROUP_PASSES = GROUP_HEADS * ROPE // K_PASS
-GROUP_WORDS = GROUP_HEADS * ROPE // PACK
+CHUNK_HEADS = 4
+CHUNKS_IN_K = HEADS // CHUNK_HEADS
+CHUNK = CHUNK_HEADS * HEAD_DIM
+CHUNK_NOPE = CHUNK_HEADS * NOPE
+CHUNK_PASSES = CHUNK // K_PASS
+NOPE_PASSES = CHUNK_NOPE // K_PASS
+PASSES = K_ALL // K_PASS
 HEAD_WORDS = ROPE // PACK
 HALF_WORDS = HALF // PACK
-QUAD = 4
+ROPE_WORDS = CHUNK_HEADS * HEAD_WORDS
+
+TOKEN_CHUNKS = TOKEN_TILES * CHUNKS_IN_K
+WEIGHT_CHUNKS = HIDDEN_TILES * CHUNKS_IN_K
+RUN = 2
+MX_LAG = 2
+LOAD_AHEAD = 3
 
 FLOPS = 2 * TOKENS * HIDDEN * K_ALL
 BYTES = 2 * (TOKENS * K_ALL + HIDDEN * K_ALL + 2 * TOKENS * ROPE) + 4 * TOKENS * HIDDEN
 
 
-def load_in_k_order(nc, dest, rows):
-    nc.sync.dma_start(
-        out=dest[:, 0:NOPE_ALL].rearrange("p (h d) -> p h d", h=HEADS),
-        in_=rows[:, :, 0:NOPE],
-    )
-    nc.sync.dma_start(
-        out=dest[:, NOPE_ALL:K_ALL].rearrange("p (h d) -> p h d", h=HEADS),
-        in_=rows[:, :, NOPE:HEAD_DIM],
-    )
-
-
-def words_of_passes(raw, passes):
-    words = raw[:].bitcast(F32)[:, 0 : passes * K_PASS // 2]
-    return words.rearrange("q (c p u) -> q c u p", c=passes, u=2)
+def words_of_passes(raw):
+    return raw[:].bitcast(F32).rearrange("q (c p u) -> q c u p", c=CHUNK_PASSES, u=2)
 
 
 def tile_gptossmlaattention_pb_k_kernel(
@@ -65,123 +57,124 @@ def tile_gptossmlaattention_pb_k_kernel(
     nc = tc.nc
     with ExitStack() as ctx:
         keep = ctx.enter_context(tc.tile_pool(name="keep", bufs=1))
-        raw_w = ctx.enter_context(tc.tile_pool(name="raw_w", bufs=2))
-        raw_g = ctx.enter_context(tc.tile_pool(name="raw_g", bufs=3))
+        raw_chunks = ctx.enter_context(tc.tile_pool(name="raw_chunks", bufs=8))
         tables = ctx.enter_context(tc.tile_pool(name="tables", bufs=2))
-        products = ctx.enter_context(tc.tile_pool(name="products", bufs=2))
-        regrouped = ctx.enter_context(tc.tile_pool(name="regrouped", bufs=3))
-        quantised = ctx.enter_context(tc.tile_pool(name="quantised", bufs=2))
+        products = ctx.enter_context(tc.tile_pool(name="products", bufs=3))
+        w_regrouped = ctx.enter_context(tc.tile_pool(name="w_regrouped", bufs=3))
+        g_regrouped = ctx.enter_context(tc.tile_pool(name="g_regrouped", bufs=2))
+        quantised = ctx.enter_context(tc.tile_pool(name="quantised", bufs=3))
         results = ctx.enter_context(tc.tile_pool(name="results", bufs=2))
         turned_banks = ctx.enter_context(tc.psum_pool(name="turned_banks", bufs=6))
         sum_banks = ctx.enter_context(tc.psum_pool(name="sum_banks", bufs=2))
+        ctx.enter_context(tc.manual_schedule())
 
         ident = keep.tile([P, P], F32)
         masks.make_identity(nc, ident[:])
         w_codes = keep.tile([P, PASSES * HIDDEN], U32, align_bytes=64)
         w_scales = keep.tile([P, PASSES * HIDDEN], U8, align_bytes=64)
 
-        def quantise_weights(it):
-            w_raw = raw_w.tile([P, K_ALL], BF16)
-            load_in_k_order(
-                nc, w_raw, Wq[it * P : (it + 1) * P, :].rearrange("i (h d) -> i h d", h=HEADS)
+        def load_chunk(rows):
+            raw = raw_chunks.tile([P, CHUNK], BF16)
+            nc.sync.dma_start(
+                out=raw[:, 0:CHUNK_NOPE].rearrange("p (h d) -> p h d", h=CHUNK_HEADS),
+                in_=rows[:, :, 0:NOPE],
             )
-            w_words = words_of_passes(w_raw, PASSES)
-            for c0 in range(0, PASSES, 2):
-                turned = turned_banks.tile([P, PACK, P], F32, tag="turned")
-                for cc in range(2):
-                    for u in range(2):
-                        nc.tensor.transpose(
-                            out=turned[:, 2 * cc + u, :],
-                            in_=w_words[:, c0 + cc, u, :],
-                            identity=ident[:],
-                        )
-                w_grouped = regrouped.tile([P, 2 * P * PACK], BF16, align_bytes=64)
+            nc.sync.dma_start(
+                out=raw[:, CHUNK_NOPE:CHUNK].rearrange("p (h d) -> p h d", h=CHUNK_HEADS),
+                in_=rows[:, :, NOPE:HEAD_DIM],
+            )
+            return raw
+
+        def turn_words(words, first_pass):
+            turned = turned_banks.tile([P, PACK, P], F32, tag="turned")
+            for cc in range(2):
+                for u in range(2):
+                    nc.tensor.transpose(
+                        out=turned[:, 2 * cc + u, :],
+                        in_=words[:, first_pass + cc, u, :],
+                        identity=ident[:],
+                    )
+            return turned[:].rearrange("p (c u) r -> p c r u", u=2)
+
+        def load_weights(w):
+            it, half = w // CHUNKS_IN_K, w % CHUNKS_IN_K
+            return load_chunk(
+                Wq[it * P : (it + 1) * P, half * CHUNK : (half + 1) * CHUNK].rearrange(
+                    "i (h d) -> i h d", h=CHUNK_HEADS
+                )
+            )
+
+        def quantise_weights(w, w_raw):
+            it, half = w // CHUNKS_IN_K, w % CHUNKS_IN_K
+            w_words = words_of_passes(w_raw)
+            for c0 in range(0, CHUNK_PASSES, 2):
+                w_grouped = w_regrouped.tile([P, 2 * K_PASS], BF16, align_bytes=64)
                 nc.scalar.copy(
                     out=w_grouped[:].bitcast(F32).rearrange("p (c i u) -> p c i u", c=2, u=2),
-                    in_=turned[:].rearrange("p (c u) i -> p c i u", u=2),
+                    in_=turn_words(w_words, c0),
                 )
                 for cc in range(2):
-                    cols = slice((c0 + cc) * HIDDEN + it * P, (c0 + cc) * HIDDEN + (it + 1) * P)
+                    first = (half * CHUNK_PASSES + c0 + cc) * HIDDEN + it * P
                     nc.vector.quantize_mx(
-                        out=w_codes[:, cols].bitcast(E4M3_X4),
-                        scales=w_scales[:, cols],
-                        in_=w_grouped[:, cc * P * PACK : (cc + 1) * P * PACK],
+                        out=w_codes[:, first : first + P].bitcast(E4M3_X4),
+                        scales=w_scales[:, first : first + P],
+                        in_=w_grouped[:, cc * K_PASS : (cc + 1) * K_PASS],
                     )
 
-        def rope_products(g_raw, cos_t, signed_sin, group):
-            heads = slice(group * GROUP_HEADS, (group + 1) * GROUP_HEADS)
-            rotated = g_raw[:, NOPE_ALL:K_ALL]
-            direct = products.tile([P, PACK, GROUP_WORDS], F32)
-            nc.vector.tensor_tensor(
-                out=direct[:].rearrange("q t (h j) -> q h t j", h=GROUP_HEADS),
-                in0=rotated.rearrange("q (h j t) -> q h t j", h=HEADS, t=PACK)[:, heads],
-                in1=cos_t[:]
-                .rearrange("q (j t) -> q t j", t=PACK)
-                .unsqueeze(1)
-                .to_broadcast([P, GROUP_HEADS, PACK, HEAD_WORDS]),
-                op=MULT,
-            )
-            crossed = products.tile([P, PACK, GROUP_WORDS], F32)
-            for f in range(2):
-                nc.vector.tensor_tensor(
-                    out=crossed[:].rearrange("q t (h f j) -> q f h t j", h=GROUP_HEADS, f=2)[:, f],
-                    in0=rotated.rearrange("q (h f j t) -> q f h t j", h=HEADS, f=2, t=PACK)[
-                        :, 1 - f, heads
-                    ],
-                    in1=signed_sin[:]
-                    .rearrange("q (f j t) -> q f t j", f=2, t=PACK)[:, 1 - f]
-                    .unsqueeze(1)
-                    .to_broadcast([P, GROUP_HEADS, PACK, HALF_WORDS]),
-                    op=MULT,
-                )
-            return direct, crossed
-
-        def quantise_tokens(n):
+        def load_tables(n):
             rows = slice(n * P, (n + 1) * P)
             cos_t = tables.tile([P, ROPE], BF16)
             nc.sync.dma_start(out=cos_t[:], in_=cos[0, rows, :])
             signed_sin = tables.tile([P, ROPE], BF16)
             nc.sync.dma_start(out=signed_sin[:], in_=sin[0, rows, :])
-            g_raw = raw_g.tile([P, K_ALL], BF16)
-            load_in_k_order(nc, g_raw, grad_out[0, :, rows, :].rearrange("h s d -> s h d"))
-            nc.scalar.mul(out=signed_sin[:, 0:HALF], in_=signed_sin[:, 0:HALF], mul=-1.0)
+            return cos_t, signed_sin
 
-            g_codes = quantised.tile([P, PASSES * P], U32, align_bytes=64)
-            g_scales = quantised.tile([P, PASSES * P], U8, align_bytes=64)
+        def load_tokens(k):
+            n, half = k // CHUNKS_IN_K, k % CHUNKS_IN_K
+            return load_chunk(
+                grad_out[
+                    0, half * CHUNK_HEADS : (half + 1) * CHUNK_HEADS, n * P : (n + 1) * P, :
+                ].rearrange("h s d -> s h d")
+            )
 
-            def quantise_quad(grouped, first_pass):
-                cols = slice(first_pass * P, (first_pass + QUAD) * P)
-                nc.vector.quantize_mx(
-                    out=g_codes[:, cols].bitcast(E5M2_X4),
-                    scales=g_scales[:, cols],
-                    in_=grouped[:],
+        def rope_products(g_raw, cos_t, signed_sin):
+            rotated = g_raw[:, CHUNK_NOPE:CHUNK]
+            direct = products.tile([P, PACK, ROPE_WORDS], F32)
+            nc.vector.tensor_tensor(
+                out=direct[:].rearrange("q t (h j) -> q h t j", h=CHUNK_HEADS),
+                in0=rotated.rearrange("q (h j t) -> q h t j", h=CHUNK_HEADS, t=PACK),
+                in1=cos_t[:]
+                .rearrange("q (j t) -> q t j", t=PACK)
+                .unsqueeze(1)
+                .to_broadcast([P, CHUNK_HEADS, PACK, HEAD_WORDS]),
+                op=MULT,
+            )
+            crossed = products.tile([P, PACK, ROPE_WORDS], F32)
+            for f in range(2):
+                nc.vector.tensor_tensor(
+                    out=crossed[:].rearrange("q t (h f j) -> q f h t j", h=CHUNK_HEADS, f=2)[:, f],
+                    in0=rotated.rearrange("q (h f j t) -> q f h t j", h=CHUNK_HEADS, f=2, t=PACK)[
+                        :, 1 - f
+                    ],
+                    in1=signed_sin[:]
+                    .rearrange("q (f j t) -> q f t j", f=2, t=PACK)[:, 1 - f]
+                    .unsqueeze(1)
+                    .to_broadcast([P, CHUNK_HEADS, PACK, HALF_WORDS]),
+                    op=MULT,
                 )
+            return direct, crossed
 
-            g_words = words_of_passes(g_raw, NOPE_PASSES)
-            grouped = regrouped.tile([P, QUAD * P * PACK], BF16, align_bytes=64)
-            for c0 in range(0, NOPE_PASSES, 2):
-                turned = turned_banks.tile([P, PACK, P], F32, tag="turned")
-                for cc in range(2):
-                    for u in range(2):
-                        nc.tensor.transpose(
-                            out=turned[:, 2 * cc + u, :],
-                            in_=g_words[:, c0 + cc, u, :],
-                            identity=ident[:],
-                        )
+        def turn_pair(first_pass, g_raw, direct, crossed, g_grouped):
+            if first_pass < NOPE_PASSES:
                 nc.scalar.copy(
-                    out=grouped[:, c0 * P * PACK : (c0 + 2) * P * PACK]
+                    out=g_grouped[:, first_pass * K_PASS : (first_pass + 2) * K_PASS]
                     .bitcast(F32)
                     .rearrange("p (c r u) -> p c r u", c=2, u=2),
-                    in_=turned[:].rearrange("p (c u) r -> p c r u", u=2),
+                    in_=turn_words(words_of_passes(g_raw), first_pass),
                 )
-            quantise_quad(grouped, 0)
-
-            for cr in range(ROPE_PASSES):
-                if cr % GROUP_PASSES == 0:
-                    direct, crossed = rope_products(g_raw, cos_t, signed_sin, cr // GROUP_PASSES)
-                if cr % QUAD == 0:
-                    grouped = regrouped.tile([P, QUAD * P * PACK], BF16, align_bytes=64)
-                block = slice((cr % GROUP_PASSES) * P, (cr % GROUP_PASSES + 1) * P)
+                return
+            for c in range(first_pass, first_pass + 2):
+                block = slice((c - NOPE_PASSES) * P, (c - NOPE_PASSES + 1) * P)
                 turned = turned_banks.tile([P, PACK, P], F32, tag="turned")
                 for t in range(PACK):
                     nc.tensor.matmul(
@@ -201,36 +194,101 @@ def tile_gptossmlaattention_pb_k_kernel(
                         stop=True,
                     )
                 nc.scalar.copy(
-                    out=grouped[:, (cr % QUAD) * P * PACK : (cr % QUAD + 1) * P * PACK].rearrange(
+                    out=g_grouped[:, c * K_PASS : (c + 1) * K_PASS].rearrange(
                         "p (r t) -> p r t", t=PACK
                     ),
                     in_=turned[:].rearrange("p t r -> p r t"),
                 )
-                if cr % QUAD == QUAD - 1:
-                    quantise_quad(grouped, NOPE_PASSES + cr - (QUAD - 1))
+
+        def quantise_tokens(g_grouped):
+            g_codes = quantised.tile([P, CHUNK_PASSES * P], U32, align_bytes=64)
+            g_scales = quantised.tile([P, CHUNK_PASSES * P], U8, align_bytes=64)
+            nc.vector.quantize_mx(
+                out=g_codes[:].bitcast(E5M2_X4), scales=g_scales[:], in_=g_grouped[:]
+            )
             return g_codes, g_scales
 
-        def multiply(n, g_codes, g_scales):
-            sums = sum_banks.tile([P, HIDDEN], F32)
-            for c in range(PASSES):
+        def multiply_passes(k, first_pass, g_codes, g_scales, sums):
+            half = k % CHUNKS_IN_K
+            for c in range(first_pass, first_pass + RUN):
+                w_cols = slice(
+                    (half * CHUNK_PASSES + c) * HIDDEN, (half * CHUNK_PASSES + c + 1) * HIDDEN
+                )
                 nc.tensor.matmul_mx(
                     out=sums[:],
                     lhsT=g_codes[:, c * P : (c + 1) * P].bitcast(E5M2_X4),
                     lhsT_scale=g_scales[:, c * P : (c + 1) * P],
-                    rhs=w_codes[:, c * HIDDEN : (c + 1) * HIDDEN].bitcast(E4M3_X4),
-                    rhs_scale=w_scales[:, c * HIDDEN : (c + 1) * HIDDEN],
-                    start=(c == 0),
-                    stop=(c == PASSES - 1),
+                    rhs=w_codes[:, w_cols].bitcast(E4M3_X4),
+                    rhs_scale=w_scales[:, w_cols],
+                    start=(half == 0 and c == 0),
+                    stop=(half == CHUNKS_IN_K - 1 and c == CHUNK_PASSES - 1),
                 )
+
+        def store_sums(n, sums):
             result = results.tile([P, HIDDEN], F32)
             nc.scalar.copy(out=result[:], in_=sums[:])
             nc.sync.dma_start(out=out[0, n * P : (n + 1) * P, :], in_=result[:])
 
-        ready = quantise_tokens(0)
-        for it in range(HIDDEN_TILES):
-            quantise_weights(it)
-        for n in range(1, TOKEN_TILES):
-            following = quantise_tokens(n)
-            multiply(n - 1, ready[0], ready[1])
-            ready = following
-        multiply(TOKEN_TILES - 1, ready[0], ready[1])
+        g_raws, g_tables, g_products, g_groupeds, g_quantised, g_sums = {}, {}, {}, {}, {}, {}
+
+        def fetch(k):
+            if k < TOKEN_CHUNKS:
+                if k % CHUNKS_IN_K == 0:
+                    g_tables[k // CHUNKS_IN_K] = load_tables(k // CHUNKS_IN_K)
+                g_raws[k] = load_tokens(k)
+
+        def multiply_by_tables(k):
+            if k < TOKEN_CHUNKS:
+                cos_t, signed_sin = g_tables[k // CHUNKS_IN_K]
+                if k % CHUNKS_IN_K == 0:
+                    nc.scalar.mul(out=signed_sin[:, 0:HALF], in_=signed_sin[:, 0:HALF], mul=-1.0)
+                g_products[k] = rope_products(g_raws[k], cos_t, signed_sin)
+
+        def step(j):
+            multiply_by_tables(j + 1)
+            if 1 <= j <= TOKEN_CHUNKS:
+                g_quantised[j - 1] = quantise_tokens(g_groupeds[j - 1])
+            k = j - MX_LAG
+            if j < TOKEN_CHUNKS:
+                g_grouped = g_regrouped.tile([P, CHUNK], BF16, align_bytes=64)
+                g_groupeds[j] = g_grouped
+            if k >= 0 and k % CHUNKS_IN_K == 0:
+                sums = sum_banks.tile([P, HIDDEN], F32)
+                g_sums[k // CHUNKS_IN_K] = sums
+            for first_pass in range(0, CHUNK_PASSES, RUN):
+                if j < TOKEN_CHUNKS:
+                    for c0 in range(first_pass, first_pass + RUN, 2):
+                        turn_pair(c0, g_raws[j], g_products[j][0], g_products[j][1], g_groupeds[j])
+                if k >= 0:
+                    multiply_passes(
+                        k, first_pass, g_quantised[k][0], g_quantised[k][1], g_sums[k // CHUNKS_IN_K]
+                    )
+            if k >= 0 and k % CHUNKS_IN_K == CHUNKS_IN_K - 1:
+                store_sums(k // CHUNKS_IN_K, g_sums[k // CHUNKS_IN_K])
+
+        w_raws = {}
+        fetch(0)
+        w_raws[0] = load_weights(0)
+        w_raws[1] = load_weights(1)
+        fetch(1)
+        w_raws[2] = load_weights(2)
+        w_raws[3] = load_weights(3)
+        fetch(2)
+        w_raws[4] = load_weights(4)
+        multiply_by_tables(0)
+        quantise_weights(0, w_raws[0])
+        quantise_weights(1, w_raws[1])
+        w_raws[5] = load_weights(5)
+        w_raws[6] = load_weights(6)
+        step(0)
+        w_raws[7] = load_weights(7)
+        quantise_weights(2, w_raws[2])
+        quantise_weights(3, w_raws[3])
+        fetch(3)
+        fetch(4)
+        step(1)
+        for w in range(4, WEIGHT_CHUNKS):
+            quantise_weights(w, w_raws[w])
+        for j in range(2, TOKEN_CHUNKS + MX_LAG):
+            fetch(j + LOAD_AHEAD)
+            step(j)

@@ -173,10 +173,13 @@ def tile_gptossmlaattention_pb_k_kernel(
                     in_=turn_words(words_of_passes(g_raw), first_pass),
                 )
                 return
-            for c in range(first_pass, first_pass + 2):
-                block = slice((c - NOPE_PASSES) * P, (c - NOPE_PASSES + 1) * P)
-                turned = turned_banks.tile([P, PACK, P], F32, tag="turned")
-                for t in range(PACK):
+            pair = range(first_pass, first_pass + 2)
+            blocks = [slice((c - NOPE_PASSES) * P, (c - NOPE_PASSES + 1) * P) for c in pair]
+            turned_a = turned_banks.tile([P, PACK, P], F32, tag="turned")
+            turned_b = turned_banks.tile([P, PACK, P], F32, tag="turned")
+            banks = [turned_a, turned_b]
+            for t in range(PACK):
+                for turned, block in zip(banks, blocks):
                     nc.tensor.matmul(
                         out=turned[:, t, :],
                         lhsT=direct[:, t, block],
@@ -185,6 +188,7 @@ def tile_gptossmlaattention_pb_k_kernel(
                         start=True,
                         stop=False,
                     )
+                for turned, block in zip(banks, blocks):
                     nc.tensor.matmul(
                         out=turned[:, t, :],
                         lhsT=crossed[:, t, block],
@@ -193,6 +197,7 @@ def tile_gptossmlaattention_pb_k_kernel(
                         start=False,
                         stop=True,
                     )
+            for turned, c in zip(banks, pair):
                 nc.scalar.copy(
                     out=g_grouped[:, c * K_PASS : (c + 1) * K_PASS].rearrange(
                         "p (r t) -> p r t", t=PACK
@@ -267,8 +272,8 @@ def tile_gptossmlaattention_pb_k_kernel(
                 store_sums(k // CHUNKS_IN_K, g_sums[k // CHUNKS_IN_K])
 
         w_raws = {}
-        fetch(0)
         w_raws[0] = load_weights(0)
+        fetch(0)
         w_raws[1] = load_weights(1)
         fetch(1)
         w_raws[2] = load_weights(2)

@@ -39,7 +39,7 @@ ROPE_WORDS = CHUNK_HEADS * HEAD_WORDS
 
 TOKEN_CHUNKS = TOKEN_TILES * CHUNKS_IN_K
 WEIGHT_CHUNKS = HIDDEN_TILES * CHUNKS_IN_K
-RUN = 2
+RUN = 4
 MX_LAG = 2
 LOAD_AHEAD = 3
 

@@ -42,6 +42,8 @@ WEIGHT_CHUNKS = HIDDEN_TILES * CHUNKS_IN_K
 RUN = 4
 MX_LAG = 2
 LOAD_AHEAD = 3
+VECTOR_TABLE = 1024
+VECTOR_WORDS = (VECTOR_TABLE - ROPE) // PACK
 
 FLOPS = 2 * TOKENS * HIDDEN * K_ALL
 BYTES = 2 * (TOKENS * K_ALL + HIDDEN * K_ALL + 2 * TOKENS * ROPE) + 4 * TOKENS * HIDDEN
@@ -58,18 +60,21 @@ def tile_gptossmlaattention_pb_k_kernel(
     with ExitStack() as ctx:
         keep = ctx.enter_context(tc.tile_pool(name="keep", bufs=1))
         raw_chunks = ctx.enter_context(tc.tile_pool(name="raw_chunks", bufs=8))
-        tables = ctx.enter_context(tc.tile_pool(name="tables", bufs=2))
+        tables = ctx.enter_context(tc.tile_pool(name="tables", bufs=4))
         products = ctx.enter_context(tc.tile_pool(name="products", bufs=3))
         w_regrouped = ctx.enter_context(tc.tile_pool(name="w_regrouped", bufs=3))
         g_regrouped = ctx.enter_context(tc.tile_pool(name="g_regrouped", bufs=2))
         quantised = ctx.enter_context(tc.tile_pool(name="quantised", bufs=3))
         results = ctx.enter_context(tc.tile_pool(name="results", bufs=2))
-        turned_banks = ctx.enter_context(tc.psum_pool(name="turned_banks", bufs=6))
-        sum_banks = ctx.enter_context(tc.psum_pool(name="sum_banks", bufs=2))
+        turned_banks = ctx.enter_context(tc.psum_pool(name="turned_banks", bufs=5))
+        sum_banks = ctx.enter_context(tc.psum_pool(name="sum_banks", bufs=1))
+        table_banks = ctx.enter_context(tc.psum_pool(name="table_banks", bufs=2))
         ctx.enter_context(tc.manual_schedule())
 
         ident = keep.tile([P, P], F32)
         masks.make_identity(nc, ident[:])
+        ident_bf = keep.tile([P, P], BF16)
+        masks.make_identity(nc, ident_bf[:])
         w_codes = keep.tile([P, PASSES * HIDDEN], U32, align_bytes=64)
         w_scales = keep.tile([P, PASSES * HIDDEN], U8, align_bytes=64)
 
@@ -121,13 +126,38 @@ def tile_gptossmlaattention_pb_k_kernel(
                         in_=w_grouped[:, cc * K_PASS : (cc + 1) * K_PASS],
                     )
 
+        g_raws, g_tables, g_banks, g_products, g_groupeds, g_quantised, g_sums = (
+            {},
+            {},
+            {},
+            {},
+            {},
+            {},
+            {},
+        )
+
         def load_tables(n):
             rows = slice(n * P, (n + 1) * P)
-            cos_t = tables.tile([P, ROPE], BF16)
-            nc.sync.dma_start(out=cos_t[:], in_=cos[0, rows, :])
-            signed_sin = tables.tile([P, ROPE], BF16)
-            nc.sync.dma_start(out=signed_sin[:], in_=sin[0, rows, :])
-            return cos_t, signed_sin
+            table = tables.tile([P, 2 * ROPE], BF16)
+            nc.sync.dma_start(out=table[:, 0:ROPE], in_=cos[0, rows, :])
+            nc.sync.dma_start(out=table[:, ROPE : 2 * ROPE], in_=sin[0, rows, :])
+            return table
+
+        def prepare_tables(n):
+            table = g_tables[n]
+            nc.scalar.mul(
+                out=table[:, ROPE : ROPE + HALF], in_=table[:, ROPE : ROPE + HALF], mul=-1.0
+            )
+            bank = table_banks.tile([P, VECTOR_TABLE], BF16)
+            for first in range(0, VECTOR_TABLE, HIDDEN):
+                nc.tensor.matmul(
+                    out=bank[:, first : first + HIDDEN],
+                    lhsT=ident_bf[:],
+                    rhs=table[:, first : first + HIDDEN],
+                    start=True,
+                    stop=True,
+                )
+            g_banks[n] = bank
 
         def load_tokens(k):
             n, half = k // CHUNKS_IN_K, k % CHUNKS_IN_K
@@ -137,31 +167,45 @@ def tile_gptossmlaattention_pb_k_kernel(
                 ].rearrange("h s d -> s h d")
             )
 
-        def rope_products(g_raw, cos_t, signed_sin):
+        def rope_products(g_raw, table, bank):
             rotated = g_raw[:, CHUNK_NOPE:CHUNK]
             direct = products.tile([P, PACK, ROPE_WORDS], F32)
             nc.vector.tensor_tensor(
                 out=direct[:].rearrange("q t (h j) -> q h t j", h=CHUNK_HEADS),
                 in0=rotated.rearrange("q (h j t) -> q h t j", h=CHUNK_HEADS, t=PACK),
-                in1=cos_t[:]
+                in1=bank[:, 0:ROPE]
                 .rearrange("q (j t) -> q t j", t=PACK)
                 .unsqueeze(1)
                 .to_broadcast([P, CHUNK_HEADS, PACK, HEAD_WORDS]),
                 op=MULT,
             )
             crossed = products.tile([P, PACK, ROPE_WORDS], F32)
-            for f in range(2):
-                nc.vector.tensor_tensor(
-                    out=crossed[:].rearrange("q t (h f j) -> q f h t j", h=CHUNK_HEADS, f=2)[:, f],
-                    in0=rotated.rearrange("q (h f j t) -> q f h t j", h=CHUNK_HEADS, f=2, t=PACK)[
-                        :, 1 - f
-                    ],
-                    in1=signed_sin[:]
-                    .rearrange("q (f j t) -> q f t j", f=2, t=PACK)[:, 1 - f]
-                    .unsqueeze(1)
-                    .to_broadcast([P, CHUNK_HEADS, PACK, HALF_WORDS]),
-                    op=MULT,
-                )
+            result = crossed[:].rearrange("q t (h f j) -> q f h t j", h=CHUNK_HEADS, f=2)
+            source = rotated.rearrange("q (h f j t) -> q f h t j", h=CHUNK_HEADS, f=2, t=PACK)
+            sines = table[:, ROPE : 2 * ROPE].rearrange("q (f j t) -> q f t j", f=2, t=PACK)
+            nc.vector.tensor_tensor(
+                out=result[:, 1, :, :, 0:VECTOR_WORDS],
+                in0=source[:, 0, :, :, 0:VECTOR_WORDS],
+                in1=bank[:, ROPE:VECTOR_TABLE]
+                .rearrange("q (j t) -> q t j", t=PACK)
+                .unsqueeze(1)
+                .to_broadcast([P, CHUNK_HEADS, PACK, VECTOR_WORDS]),
+                op=MULT,
+            )
+            nc.gpsimd.tensor_tensor(
+                out=result[:, 0],
+                in0=source[:, 1],
+                in1=sines[:, 1].unsqueeze(1).to_broadcast([P, CHUNK_HEADS, PACK, HALF_WORDS]),
+                op=MULT,
+            )
+            nc.gpsimd.tensor_tensor(
+                out=result[:, 1, :, :, VECTOR_WORDS:HALF_WORDS],
+                in0=source[:, 0, :, :, VECTOR_WORDS:HALF_WORDS],
+                in1=sines[:, 0, :, VECTOR_WORDS:HALF_WORDS]
+                .unsqueeze(1)
+                .to_broadcast([P, CHUNK_HEADS, PACK, HALF_WORDS - VECTOR_WORDS]),
+                op=MULT,
+            )
             return direct, crossed
 
         def turn_pair(first_pass, g_raw, direct, crossed, g_grouped):
@@ -234,20 +278,19 @@ def tile_gptossmlaattention_pb_k_kernel(
             nc.scalar.copy(out=result[:], in_=sums[:])
             nc.sync.dma_start(out=out[0, n * P : (n + 1) * P, :], in_=result[:])
 
-        g_raws, g_tables, g_products, g_groupeds, g_quantised, g_sums = {}, {}, {}, {}, {}, {}
-
         def fetch(k):
             if k < TOKEN_CHUNKS:
-                if k % CHUNKS_IN_K == 0:
-                    g_tables[k // CHUNKS_IN_K] = load_tables(k // CHUNKS_IN_K)
+                if k == 0:
+                    g_tables[0] = load_tables(0)
                 g_raws[k] = load_tokens(k)
+                n = (k + 1) // CHUNKS_IN_K
+                if k % CHUNKS_IN_K == 1 and n < TOKEN_TILES:
+                    g_tables[n] = load_tables(n)
 
         def multiply_by_tables(k):
             if k < TOKEN_CHUNKS:
-                cos_t, signed_sin = g_tables[k // CHUNKS_IN_K]
-                if k % CHUNKS_IN_K == 0:
-                    nc.scalar.mul(out=signed_sin[:, 0:HALF], in_=signed_sin[:, 0:HALF], mul=-1.0)
-                g_products[k] = rope_products(g_raws[k], cos_t, signed_sin)
+                n = k // CHUNKS_IN_K
+                g_products[k] = rope_products(g_raws[k], g_tables[n], g_banks[n])
 
         def step(j):
             multiply_by_tables(j + 1)
@@ -268,6 +311,8 @@ def tile_gptossmlaattention_pb_k_kernel(
                     multiply_passes(
                         k, first_pass, g_quantised[k][0], g_quantised[k][1], g_sums[k // CHUNKS_IN_K]
                     )
+                if first_pass == 0 and j % CHUNKS_IN_K == 1 and (j + 3) // CHUNKS_IN_K < TOKEN_TILES:
+                    prepare_tables((j + 3) // CHUNKS_IN_K)
             if k >= 0 and k % CHUNKS_IN_K == CHUNKS_IN_K - 1:
                 store_sums(k // CHUNKS_IN_K, g_sums[k // CHUNKS_IN_K])
 
@@ -280,9 +325,11 @@ def tile_gptossmlaattention_pb_k_kernel(
         w_raws[3] = load_weights(3)
         fetch(2)
         w_raws[4] = load_weights(4)
+        prepare_tables(0)
         multiply_by_tables(0)
         quantise_weights(0, w_raws[0])
         quantise_weights(1, w_raws[1])
+        prepare_tables(1)
         w_raws[5] = load_weights(5)
         w_raws[6] = load_weights(6)
         step(0)

@@ -77,6 +77,7 @@ def tile_gptossmlaattention_pb_k_kernel(
         masks.make_identity(nc, ident_bf[:])
         w_codes = keep.tile([P, PASSES * HIDDEN], U32, align_bytes=64)
         w_scales = keep.tile([P, PASSES * HIDDEN], U8, align_bytes=64)
+        gate_word = keep.tile([P, 1], U32)
 
         def load_chunk(rows):
             raw = raw_chunks.tile([P, CHUNK], BF16)
@@ -290,6 +291,8 @@ def tile_gptossmlaattention_pb_k_kernel(
         def multiply_by_tables(k):
             if k < TOKEN_CHUNKS:
                 n = k // CHUNKS_IN_K
+                if k - 3 in g_quantised:
+                    nc.gpsimd.tensor_copy(out=gate_word[:], in_=g_quantised[k - 3][0][:, 0:1])
                 g_products[k] = rope_products(g_raws[k], g_tables[n], g_banks[n])
 
         def step(j):

@@ -39,7 +39,7 @@ ROPE_WORDS = CHUNK_HEADS * HEAD_WORDS
 
 TOKEN_CHUNKS = TOKEN_TILES * CHUNKS_IN_K
 WEIGHT_CHUNKS = HIDDEN_TILES * CHUNKS_IN_K
-RUN = 4
+RUN = 8
 MX_LAG = 2
 LOAD_AHEAD = 3
 VECTOR_TABLE = 1024

@@ -66,6 +66,7 @@ def tile_gptossmlaattention_pb_k_kernel(
         g_regrouped = ctx.enter_context(tc.tile_pool(name="g_regrouped", bufs=2))
         quantised = ctx.enter_context(tc.tile_pool(name="quantised", bufs=3))
         results = ctx.enter_context(tc.tile_pool(name="results", bufs=2))
+        sorted_words = ctx.enter_context(tc.tile_pool(name="sorted_words", bufs=2))
         turned_banks = ctx.enter_context(tc.psum_pool(name="turned_banks", bufs=5))
         sum_banks = ctx.enter_context(tc.psum_pool(name="sum_banks", bufs=1))
         table_banks = ctx.enter_context(tc.psum_pool(name="table_banks", bufs=2))
@@ -127,7 +128,8 @@ def tile_gptossmlaattention_pb_k_kernel(
                         in_=w_grouped[:, cc * K_PASS : (cc + 1) * K_PASS],
                     )
 
-        g_raws, g_tables, g_banks, g_products, g_groupeds, g_quantised, g_sums = (
+        g_raws, g_sorted, g_tables, g_banks, g_products, g_groupeds, g_quantised, g_sums = (
+            {},
             {},
             {},
             {},
@@ -209,13 +211,24 @@ def tile_gptossmlaattention_pb_k_kernel(
             )
             return direct, crossed
 
+        def sort_unrotated(k):
+            if k < TOKEN_CHUNKS:
+                in_order = sorted_words.tile([P, CHUNK_NOPE // 2], F32)
+                nc.scalar.copy(
+                    out=in_order[:].rearrange("q (c u p) -> q c u p", c=NOPE_PASSES, u=2),
+                    in_=words_of_passes(g_raws[k])[:, 0:NOPE_PASSES],
+                )
+                g_sorted[k] = in_order
+
         def turn_pair(first_pass, g_raw, direct, crossed, g_grouped):
             if first_pass < NOPE_PASSES:
                 nc.scalar.copy(
                     out=g_grouped[:, first_pass * K_PASS : (first_pass + 2) * K_PASS]
                     .bitcast(F32)
                     .rearrange("p (c r u) -> p c r u", c=2, u=2),
-                    in_=turn_words(words_of_passes(g_raw), first_pass),
+                    in_=turn_words(
+                        g_raw[:].rearrange("q (c u p) -> q c u p", c=NOPE_PASSES, u=2), first_pass
+                    ),
                 )
                 return
             pair = range(first_pass, first_pass + 2)
@@ -309,7 +322,10 @@ def tile_gptossmlaattention_pb_k_kernel(
             for first_pass in range(0, CHUNK_PASSES, RUN):
                 if j < TOKEN_CHUNKS:
                     for c0 in range(first_pass, first_pass + RUN, 2):
-                        turn_pair(c0, g_raws[j], g_products[j][0], g_products[j][1], g_groupeds[j])
+                        turn_pair(
+                            c0, g_sorted[j], g_products[j][0], g_products[j][1], g_groupeds[j]
+                        )
+                    sort_unrotated(j + 1)
                 if k >= 0:
                     multiply_passes(
                         k, first_pass, g_quantised[k][0], g_quantised[k][1], g_sums[k // CHUNKS_IN_K]
@@ -333,6 +349,7 @@ def tile_gptossmlaattention_pb_k_kernel(
         quantise_weights(0, w_raws[0])
         quantise_weights(1, w_raws[1])
         prepare_tables(1)
+        sort_unrotated(0)
         w_raws[5] = load_weights(5)
         w_raws[6] = load_weights(6)
         step(0)

@@ -38,7 +38,9 @@ HALF_WORDS = HALF // PACK
 ROPE_WORDS = CHUNK_HEADS * HEAD_WORDS
 
 TOKEN_CHUNKS = TOKEN_TILES * CHUNKS_IN_K
-WEIGHT_CHUNKS = HIDDEN_TILES * CHUNKS_IN_K
+PAIR = 2 * K_PASS
+CHUNK_PAIRS = CHUNK // PAIR
+WEIGHT_CHUNKS = K_ALL // PAIR
 RUN = 8
 MX_LAG = 2
 LOAD_AHEAD = 3
@@ -62,8 +64,7 @@ def tile_gptossmlaattention_pb_k_kernel(
         raw_chunks = ctx.enter_context(tc.tile_pool(name="raw_chunks", bufs=8))
         tables = ctx.enter_context(tc.tile_pool(name="tables", bufs=4))
         products = ctx.enter_context(tc.tile_pool(name="products", bufs=3))
-        w_regrouped = ctx.enter_context(tc.tile_pool(name="w_regrouped", bufs=3))
-        g_regrouped = ctx.enter_context(tc.tile_pool(name="g_regrouped", bufs=2))
+        regrouped = ctx.enter_context(tc.tile_pool(name="regrouped", bufs=3))
         quantised = ctx.enter_context(tc.tile_pool(name="quantised", bufs=3))
         results = ctx.enter_context(tc.tile_pool(name="results", bufs=2))
         sorted_words = ctx.enter_context(tc.tile_pool(name="sorted_words", bufs=2))
@@ -79,6 +80,7 @@ def tile_gptossmlaattention_pb_k_kernel(
         w_codes = keep.tile([P, PASSES * HIDDEN], U32, align_bytes=64)
         w_scales = keep.tile([P, PASSES * HIDDEN], U8, align_bytes=64)
         gate_word = keep.tile([P, 1], U32)
+        latest = {}
 
         def load_chunk(rows):
             raw = raw_chunks.tile([P, CHUNK], BF16)
@@ -103,30 +105,49 @@ def tile_gptossmlaattention_pb_k_kernel(
                     )
             return turned[:].rearrange("p (c u) r -> p c r u", u=2)
 
+        def runs_of_pair(pair):
+            first, last = pair * PAIR, (pair + 1) * PAIR
+            runs = []
+            for h in range(CHUNK_HEADS):
+                for start, d0, size in ((h * NOPE, 0, NOPE), (CHUNK_NOPE + h * ROPE, NOPE, ROPE)):
+                    low, high = max(first, start), min(last, start + size)
+                    if low < high:
+                        runs.append((low - first, h, d0 + low - start, high - low))
+            return runs
+
         def load_weights(w):
-            it, half = w // CHUNKS_IN_K, w % CHUNKS_IN_K
-            return load_chunk(
-                Wq[it * P : (it + 1) * P, half * CHUNK : (half + 1) * CHUNK].rearrange(
-                    "i (h d) -> i h d", h=CHUNK_HEADS
+            half, pair = w // CHUNK_PAIRS, w % CHUNK_PAIRS
+            raw = raw_chunks.tile([P, CHUNK], BF16)
+            by_tile = raw[:].rearrange("p (i k) -> p i k", i=HIDDEN_TILES)
+            for at, h, d, size in runs_of_pair(pair):
+                k0 = (half * CHUNK_HEADS + h) * HEAD_DIM + d
+                nc.sync.dma_start(
+                    out=by_tile[:, :, at : at + size],
+                    in_=Wq[:, k0 : k0 + size].rearrange("(i p) k -> p i k", p=P),
                 )
-            )
+            return raw
 
         def quantise_weights(w, w_raw):
-            it, half = w // CHUNKS_IN_K, w % CHUNKS_IN_K
-            w_words = words_of_passes(w_raw)
-            for c0 in range(0, CHUNK_PASSES, 2):
-                w_grouped = w_regrouped.tile([P, 2 * K_PASS], BF16, align_bytes=64)
-                nc.scalar.copy(
-                    out=w_grouped[:].bitcast(F32).rearrange("p (c i u) -> p c i u", c=2, u=2),
-                    in_=turn_words(w_words, c0),
-                )
-                for cc in range(2):
-                    first = (half * CHUNK_PASSES + c0 + cc) * HIDDEN + it * P
-                    nc.vector.quantize_mx(
-                        out=w_codes[:, first : first + P].bitcast(E4M3_X4),
-                        scales=w_scales[:, first : first + P],
-                        in_=w_grouped[:, cc * K_PASS : (cc + 1) * K_PASS],
+            w_words = w_raw[:].bitcast(F32).rearrange(
+                "q (i c p u) -> q c i u p", i=HIDDEN_TILES, c=2, u=2
+            )
+            w_grouped = regrouped.tile([P, CHUNK], BF16, align_bytes=64, tag="grouped")
+            for c in range(2):
+                for i0 in range(0, HIDDEN_TILES, 2):
+                    first = (c * HIDDEN_TILES + i0) * K_PASS
+                    nc.scalar.copy(
+                        out=w_grouped[:, first : first + 2 * K_PASS]
+                        .bitcast(F32)
+                        .rearrange("p (i r u) -> p i r u", i=2, u=2),
+                        in_=turn_words(w_words[:, c], i0),
                     )
+            first = w * 2 * HIDDEN
+            nc.vector.quantize_mx(
+                out=w_codes[:, first : first + 2 * HIDDEN].bitcast(E4M3_X4),
+                scales=w_scales[:, first : first + 2 * HIDDEN],
+                in_=w_grouped[:],
+            )
+            latest["codes"] = w_codes[:, first : first + 1]
 
         g_raws, g_sorted, g_tables, g_banks, g_products, g_groupeds, g_quantised, g_sums = (
             {},
@@ -269,6 +290,7 @@ def tile_gptossmlaattention_pb_k_kernel(
             nc.vector.quantize_mx(
                 out=g_codes[:].bitcast(E5M2_X4), scales=g_scales[:], in_=g_grouped[:]
             )
+            latest["codes"] = g_codes[:, 0:1]
             return g_codes, g_scales
 
         def multiply_passes(k, first_pass, g_codes, g_scales, sums):
@@ -297,15 +319,15 @@ def tile_gptossmlaattention_pb_k_kernel(
                 if k == 0:
                     g_tables[0] = load_tables(0)
                 g_raws[k] = load_tokens(k)
-                n = (k + 1) // CHUNKS_IN_K
-                if k % CHUNKS_IN_K == 1 and n < TOKEN_TILES:
+                n = k // CHUNKS_IN_K + 1
+                if k % CHUNKS_IN_K == 0 and n < TOKEN_TILES:
                     g_tables[n] = load_tables(n)
 
         def multiply_by_tables(k):
             if k < TOKEN_CHUNKS:
                 n = k // CHUNKS_IN_K
-                if k - 3 in g_quantised:
-                    nc.gpsimd.tensor_copy(out=gate_word[:], in_=g_quantised[k - 3][0][:, 0:1])
+                if "codes" in latest:
+                    nc.gpsimd.tensor_copy(out=gate_word[:], in_=latest["codes"])
                 g_products[k] = rope_products(g_raws[k], g_tables[n], g_banks[n])
 
         def step(j):
@@ -314,7 +336,7 @@ def tile_gptossmlaattention_pb_k_kernel(
                 g_quantised[j - 1] = quantise_tokens(g_groupeds[j - 1])
             k = j - MX_LAG
             if j < TOKEN_CHUNKS:
-                g_grouped = g_regrouped.tile([P, CHUNK], BF16, align_bytes=64)
+                g_grouped = regrouped.tile([P, CHUNK], BF16, align_bytes=64, tag="grouped")
                 g_groupeds[j] = g_grouped
             if k >= 0 and k % CHUNKS_IN_K == 0:
                 sums = sum_banks.tile([P, HIDDEN], F32)

@@ -44,6 +44,7 @@ WEIGHT_CHUNKS = K_ALL // PAIR
 RUN = 8
 MX_LAG = 2
 LOAD_AHEAD = 3
+SORT_FROM = 4
 VECTOR_TABLE = 1024
 VECTOR_WORDS = (VECTOR_TABLE - ROPE) // PACK
 
@@ -135,7 +136,9 @@ def tile_gptossmlaattention_pb_k_kernel(
             for c in range(2):
                 for i0 in range(0, HIDDEN_TILES, 2):
                     first = (c * HIDDEN_TILES + i0) * K_PASS
-                    nc.scalar.copy(
+                    last_bank = c == 1 and i0 == HIDDEN_TILES - 2
+                    copy_out = nc.vector.tensor_copy if last_bank else nc.scalar.copy
+                    copy_out(
                         out=w_grouped[:, first : first + 2 * K_PASS]
                         .bitcast(F32)
                         .rearrange("p (i r u) -> p i r u", i=2, u=2),
@@ -167,11 +170,14 @@ def tile_gptossmlaattention_pb_k_kernel(
             nc.sync.dma_start(out=table[:, ROPE : 2 * ROPE], in_=sin[0, rows, :])
             return table
 
-        def prepare_tables(n):
+        def sign_tables(n):
             table = g_tables[n]
             nc.scalar.mul(
                 out=table[:, ROPE : ROPE + HALF], in_=table[:, ROPE : ROPE + HALF], mul=-1.0
             )
+
+        def copy_tables(n):
+            table = g_tables[n]
             bank = table_banks.tile([P, VECTOR_TABLE], BF16)
             for first in range(0, VECTOR_TABLE, HIDDEN):
                 nc.tensor.matmul(
@@ -233,7 +239,7 @@ def tile_gptossmlaattention_pb_k_kernel(
             return direct, crossed
 
         def sort_unrotated(k):
-            if k < TOKEN_CHUNKS:
+            if SORT_FROM <= k < TOKEN_CHUNKS:
                 in_order = sorted_words.tile([P, CHUNK_NOPE // 2], F32)
                 nc.scalar.copy(
                     out=in_order[:].rearrange("q (c u p) -> q c u p", c=NOPE_PASSES, u=2),
@@ -241,15 +247,18 @@ def tile_gptossmlaattention_pb_k_kernel(
                 )
                 g_sorted[k] = in_order
 
+        def unrotated_words(k):
+            if k in g_sorted:
+                return g_sorted[k][:].rearrange("q (c u p) -> q c u p", c=NOPE_PASSES, u=2)
+            return words_of_passes(g_raws[k])
+
         def turn_pair(first_pass, g_raw, direct, crossed, g_grouped):
             if first_pass < NOPE_PASSES:
                 nc.scalar.copy(
                     out=g_grouped[:, first_pass * K_PASS : (first_pass + 2) * K_PASS]
                     .bitcast(F32)
                     .rearrange("p (c r u) -> p c r u", c=2, u=2),
-                    in_=turn_words(
-                        g_raw[:].rearrange("q (c u p) -> q c u p", c=NOPE_PASSES, u=2), first_pass
-                    ),
+                    in_=turn_words(g_raw, first_pass),
                 )
                 return
             pair = range(first_pass, first_pass + 2)
@@ -341,19 +350,23 @@ def tile_gptossmlaattention_pb_k_kernel(
             if k >= 0 and k % CHUNKS_IN_K == 0:
                 sums = sum_banks.tile([P, HIDDEN], F32)
                 g_sums[k // CHUNKS_IN_K] = sums
+            next_tile = (j + 3) // CHUNKS_IN_K
+            new_tables = j % CHUNKS_IN_K == 1 and next_tile < TOKEN_TILES
+            if new_tables:
+                sign_tables(next_tile)
             for first_pass in range(0, CHUNK_PASSES, RUN):
                 if j < TOKEN_CHUNKS:
                     for c0 in range(first_pass, first_pass + RUN, 2):
                         turn_pair(
-                            c0, g_sorted[j], g_products[j][0], g_products[j][1], g_groupeds[j]
+                            c0, unrotated_words(j), g_products[j][0], g_products[j][1], g_groupeds[j]
                         )
                     sort_unrotated(j + 1)
                 if k >= 0:
                     multiply_passes(
                         k, first_pass, g_quantised[k][0], g_quantised[k][1], g_sums[k // CHUNKS_IN_K]
                     )
-                if first_pass == 0 and j % CHUNKS_IN_K == 1 and (j + 3) // CHUNKS_IN_K < TOKEN_TILES:
-                    prepare_tables((j + 3) // CHUNKS_IN_K)
+                if first_pass == 0 and new_tables:
+                    copy_tables(next_tile)
             if k >= 0 and k % CHUNKS_IN_K == CHUNKS_IN_K - 1:
                 store_sums(k // CHUNKS_IN_K, g_sums[k // CHUNKS_IN_K])
 
@@ -366,23 +379,24 @@ def tile_gptossmlaattention_pb_k_kernel(
         w_raws[3] = load_weights(3)
         fetch(2)
         w_raws[4] = load_weights(4)
-        prepare_tables(0)
+        sign_tables(0)
+        copy_tables(0)
         multiply_by_tables(0)
         quantise_weights(0, w_raws[0])
+        sign_tables(1)
         quantise_weights(1, w_raws[1])
-        prepare_tables(1)
-        sort_unrotated(0)
+        copy_tables(1)
         w_raws[5] = load_weights(5)
-        w_raws[6] = load_weights(6)
+        fetch(3)
         step(0)
-        w_raws[7] = load_weights(7)
+        w_raws[6] = load_weights(6)
         quantise_weights(2, w_raws[2])
         quantise_weights(3, w_raws[3])
-        fetch(3)
+        w_raws[7] = load_weights(7)
         fetch(4)
         step(1)
-        for w in range(4, WEIGHT_CHUNKS):
-            quantise_weights(w, w_raws[w])
         for j in range(2, TOKEN_CHUNKS + MX_LAG):
+            for w in range(2 * j, min(2 * j + 2, WEIGHT_CHUNKS)):
+                quantise_weights(w, w_raws[w])
             fetch(j + LOAD_AHEAD)
             step(j)

@@ -44,6 +44,7 @@ WEIGHT_CHUNKS = K_ALL // PAIR
 RUN = 8
 MX_LAG = 2
 LOAD_AHEAD = 3
+WARM_STEPS = 4
 SORT_FROM = 4
 VECTOR_TABLE = 1024
 VECTOR_WORDS = (VECTOR_TABLE - ROPE) // PACK
@@ -81,6 +82,8 @@ def tile_gptossmlaattention_pb_k_kernel(
         w_codes = keep.tile([P, PASSES * HIDDEN], U32, align_bytes=64)
         w_scales = keep.tile([P, PASSES * HIDDEN], U8, align_bytes=64)
         gate_word = keep.tile([P, 1], U32)
+        zeros = keep.tile([P, HIDDEN], BF16)
+        nc.vector.memset(zeros[:], 0.0)
         latest = {}
 
         def load_chunk(rows):
@@ -94,6 +97,17 @@ def tile_gptossmlaattention_pb_k_kernel(
                 in_=rows[:, :, NOPE:HEAD_DIM],
             )
             return raw
+
+        def keep_warm():
+            unread = turned_banks.tile([P, PACK, P], F32, tag="turned")
+            for repeat in range(2):
+                nc.tensor.matmul(
+                    out=unread[:].rearrange("p t r -> p (t r)"),
+                    lhsT=ident_bf[:],
+                    rhs=zeros[:],
+                    start=True,
+                    stop=True,
+                )
 
         def turn_words(words, first_pass):
             turned = turned_banks.tile([P, PACK, P], F32, tag="turned")
@@ -357,6 +371,8 @@ def tile_gptossmlaattention_pb_k_kernel(
             for first_pass in range(0, CHUNK_PASSES, RUN):
                 if j < TOKEN_CHUNKS:
                     for c0 in range(first_pass, first_pass + RUN, 2):
+                        if j < WARM_STEPS and c0 >= NOPE_PASSES:
+                            keep_warm()
                         turn_pair(
                             c0, unrotated_words(j), g_products[j][0], g_products[j][1], g_groupeds[j]
                         )

@@ -89,18 +89,18 @@ def tile_gptossmlaattention_pb_k_kernel(
         def load_chunk(rows):
             raw = raw_chunks.tile([P, CHUNK], BF16)
             nc.sync.dma_start(
-                out=raw[:, 0:CHUNK_NOPE].rearrange("p (h d) -> p h d", h=CHUNK_HEADS),
-                in_=rows[:, :, 0:NOPE],
-            )
-            nc.sync.dma_start(
                 out=raw[:, CHUNK_NOPE:CHUNK].rearrange("p (h d) -> p h d", h=CHUNK_HEADS),
                 in_=rows[:, :, NOPE:HEAD_DIM],
             )
+            nc.sync.dma_start(
+                out=raw[:, 0:CHUNK_NOPE].rearrange("p (h d) -> p h d", h=CHUNK_HEADS),
+                in_=rows[:, :, 0:NOPE],
+            )
             return raw
 
-        def keep_warm():
+        def keep_warm(count):
             unread = turned_banks.tile([P, PACK, P], F32, tag="turned")
-            for repeat in range(2):
+            for repeat in range(count):
                 nc.tensor.matmul(
                     out=unread[:].rearrange("p t r -> p (t r)"),
                     lhsT=ident_bf[:],
@@ -372,7 +372,7 @@ def tile_gptossmlaattention_pb_k_kernel(
                 if j < TOKEN_CHUNKS:
                     for c0 in range(first_pass, first_pass + RUN, 2):
                         if j < WARM_STEPS and c0 >= NOPE_PASSES:
-                            keep_warm()
+                            keep_warm(2 if c0 == NOPE_PASSES else 1)
                         turn_pair(
                             c0, unrotated_words(j), g_products[j][0], g_products[j][1], g_groupeds[j]
                         )
@@ -387,8 +387,8 @@ def tile_gptossmlaattention_pb_k_kernel(
                 store_sums(k // CHUNKS_IN_K, g_sums[k // CHUNKS_IN_K])
 
         w_raws = {}
-        w_raws[0] = load_weights(0)
         fetch(0)
+        w_raws[0] = load_weights(0)
         w_raws[1] = load_weights(1)
         fetch(1)
         w_raws[2] = load_weights(2)

from contextlib import ExitStack

import concourse.masks as masks
import concourse.mybir as mybir

F32 = mybir.dt.float32
BF16 = mybir.dt.bfloat16
U32 = mybir.dt.uint32
U8 = mybir.dt.uint8
E5M2_X4 = mybir.dt.float8_e5m2_x4
E4M3_X4 = mybir.dt.float8_e4m3fn_x4
MULT = mybir.AluOpType.mult

P = 128
PACK = 4
K_PASS = P * PACK

TOKENS = 1024
HIDDEN = 512
HEADS = 8
NOPE = 256
ROPE = 768
HALF = ROPE // 2
HEAD_DIM = NOPE + ROPE
K_ALL = HEADS * HEAD_DIM
TOKEN_TILES = TOKENS // P
HIDDEN_TILES = HIDDEN // P

CHUNK_HEADS = 4
CHUNKS_IN_K = HEADS // CHUNK_HEADS
CHUNK = CHUNK_HEADS * HEAD_DIM
CHUNK_NOPE = CHUNK_HEADS * NOPE
CHUNK_PASSES = CHUNK // K_PASS
NOPE_PASSES = CHUNK_NOPE // K_PASS
PASSES = K_ALL // K_PASS
HEAD_WORDS = ROPE // PACK
HALF_WORDS = HALF // PACK
ROPE_WORDS = CHUNK_HEADS * HEAD_WORDS

TOKEN_CHUNKS = TOKEN_TILES * CHUNKS_IN_K
PAIR = 2 * K_PASS
CHUNK_PAIRS = CHUNK // PAIR
WEIGHT_CHUNKS = K_ALL // PAIR
RUN = 8
MX_LAG = 2
LOAD_AHEAD = 3
WARM_STEPS = 4
SORT_FROM = 4
VECTOR_TABLE = 1024
VECTOR_WORDS = (VECTOR_TABLE - ROPE) // PACK

FLOPS = 2 * TOKENS * HIDDEN * K_ALL
BYTES = 2 * (TOKENS * K_ALL + HIDDEN * K_ALL + 2 * TOKENS * ROPE) + 4 * TOKENS * HIDDEN


def words_of_passes(raw):
    return raw[:].bitcast(F32).rearrange("q (c p u) -> q c u p", c=CHUNK_PASSES, u=2)


def tile_gptossmlaattention_pb_k_kernel(
    tc, hidden_states, cos, sin, Wq, bq, grad_out, out
):
    nc = tc.nc
    with ExitStack() as ctx:
        keep = ctx.enter_context(tc.tile_pool(name="keep", bufs=1))
        raw_chunks = ctx.enter_context(tc.tile_pool(name="raw_chunks", bufs=8))
        tables = ctx.enter_context(tc.tile_pool(name="tables", bufs=4))
        products = ctx.enter_context(tc.tile_pool(name="products", bufs=3))
        regrouped = ctx.enter_context(tc.tile_pool(name="regrouped", bufs=3))
        quantised = ctx.enter_context(tc.tile_pool(name="quantised", bufs=3))
        results = ctx.enter_context(tc.tile_pool(name="results", bufs=2))
        sorted_words = ctx.enter_context(tc.tile_pool(name="sorted_words", bufs=2))
        turned_banks = ctx.enter_context(tc.psum_pool(name="turned_banks", bufs=5))
        sum_banks = ctx.enter_context(tc.psum_pool(name="sum_banks", bufs=1))
        table_banks = ctx.enter_context(tc.psum_pool(name="table_banks", bufs=2))
        ctx.enter_context(tc.manual_schedule())

        ident = keep.tile([P, P], F32)
        masks.make_identity(nc, ident[:])
        ident_bf = keep.tile([P, P], BF16)
        masks.make_identity(nc, ident_bf[:])
        w_codes = keep.tile([P, PASSES * HIDDEN], U32, align_bytes=64)
        w_scales = keep.tile([P, PASSES * HIDDEN], U8, align_bytes=64)
        gate_word = keep.tile([P, 1], U32)
        zeros = keep.tile([P, HIDDEN], BF16)
        nc.vector.memset(zeros[:], 0.0)
        latest = {}

        def load_chunk(rows):
            raw = raw_chunks.tile([P, CHUNK], BF16)
            nc.sync.dma_start(
                out=raw[:, CHUNK_NOPE:CHUNK].rearrange("p (h d) -> p h d", h=CHUNK_HEADS),
                in_=rows[:, :, NOPE:HEAD_DIM],
            )
            nc.sync.dma_start(
                out=raw[:, 0:CHUNK_NOPE].rearrange("p (h d) -> p h d", h=CHUNK_HEADS),
                in_=rows[:, :, 0:NOPE],
            )
            return raw

        def keep_warm(count):
            unread = turned_banks.tile([P, PACK, P], F32, tag="turned")
            for repeat in range(count):
                nc.tensor.matmul(
                    out=unread[:].rearrange("p t r -> p (t r)"),
                    lhsT=ident_bf[:],
                    rhs=zeros[:],
                    start=True,
                    stop=True,
                )

        def turn_words(words, first_pass):
            turned = turned_banks.tile([P, PACK, P], F32, tag="turned")
            for cc in range(2):
                for u in range(2):
                    nc.tensor.transpose(
                        out=turned[:, 2 * cc + u, :],
                        in_=words[:, first_pass + cc, u, :],
                        identity=ident[:],
                    )
            return turned[:].rearrange("p (c u) r -> p c r u", u=2)

        def runs_of_pair(pair):
            first, last = pair * PAIR, (pair + 1) * PAIR
            runs = []
            for h in range(CHUNK_HEADS):
                for start, d0, size in ((h * NOPE, 0, NOPE), (CHUNK_NOPE + h * ROPE, NOPE, ROPE)):
                    low, high = max(first, start), min(last, start + size)
                    if low < high:
                        runs.append((low - first, h, d0 + low - start, high - low))
            return runs

        def load_weights(w):
            half, pair = w // CHUNK_PAIRS, w % CHUNK_PAIRS
            raw = raw_chunks.tile([P, CHUNK], BF16)
            by_tile = raw[:].rearrange("p (i k) -> p i k", i=HIDDEN_TILES)
            for at, h, d, size in runs_of_pair(pair):
                k0 = (half * CHUNK_HEADS + h) * HEAD_DIM + d
                nc.sync.dma_start(
                    out=by_tile[:, :, at : at + size],
                    in_=Wq[:, k0 : k0 + size].rearrange("(i p) k -> p i k", p=P),
                )
            return raw

        def quantise_weights(w, w_raw):
            w_words = w_raw[:].bitcast(F32).rearrange(
                "q (i c p u) -> q c i u p", i=HIDDEN_TILES, c=2, u=2
            )
            w_grouped = regrouped.tile([P, CHUNK], BF16, align_bytes=64, tag="grouped")
            for c in range(2):
                for i0 in range(0, HIDDEN_TILES, 2):
                    first = (c * HIDDEN_TILES + i0) * K_PASS
                    last_bank = c == 1 and i0 == HIDDEN_TILES - 2
                    copy_out = nc.vector.tensor_copy if last_bank else nc.scalar.copy
                    copy_out(
                        out=w_grouped[:, first : first + 2 * K_PASS]
                        .bitcast(F32)
                        .rearrange("p (i r u) -> p i r u", i=2, u=2),
                        in_=turn_words(w_words[:, c], i0),
                    )
            first = w * 2 * HIDDEN
            nc.vector.quantize_mx(
                out=w_codes[:, first : first + 2 * HIDDEN].bitcast(E4M3_X4),
                scales=w_scales[:, first : first + 2 * HIDDEN],
                in_=w_grouped[:],
            )
            latest["codes"] = w_codes[:, first : first + 1]

        g_raws, g_sorted, g_tables, g_banks, g_products, g_groupeds, g_quantised, g_sums = (
            {},
            {},
            {},
            {},
            {},
            {},
            {},
            {},
        )

        def load_tables(n):
            rows = slice(n * P, (n + 1) * P)
            table = tables.tile([P, 2 * ROPE], BF16)
            nc.sync.dma_start(out=table[:, 0:ROPE], in_=cos[0, rows, :])
            nc.sync.dma_start(out=table[:, ROPE : 2 * ROPE], in_=sin[0, rows, :])
            return table

        def sign_tables(n):
            table = g_tables[n]
            nc.scalar.mul(
                out=table[:, ROPE : ROPE + HALF], in_=table[:, ROPE : ROPE + HALF], mul=-1.0
            )

        def copy_tables(n):
            table = g_tables[n]
            bank = table_banks.tile([P, VECTOR_TABLE], BF16)
            for first in range(0, VECTOR_TABLE, HIDDEN):
                nc.tensor.matmul(
                    out=bank[:, first : first + HIDDEN],
                    lhsT=ident_bf[:],
                    rhs=table[:, first : first + HIDDEN],
                    start=True,
                    stop=True,
                )
            g_banks[n] = bank

        def load_tokens(k):
            n, half = k // CHUNKS_IN_K, k % CHUNKS_IN_K
            return load_chunk(
                grad_out[
                    0, half * CHUNK_HEADS : (half + 1) * CHUNK_HEADS, n * P : (n + 1) * P, :
                ].rearrange("h s d -> s h d")
            )

        def rope_products(g_raw, table, bank):
            rotated = g_raw[:, CHUNK_NOPE:CHUNK]
            direct = products.tile([P, PACK, ROPE_WORDS], F32)
            nc.vector.tensor_tensor(
                out=direct[:].rearrange("q t (h j) -> q h t j", h=CHUNK_HEADS),
                in0=rotated.rearrange("q (h j t) -> q h t j", h=CHUNK_HEADS, t=PACK),
                in1=bank[:, 0:ROPE]
                .rearrange("q (j t) -> q t j", t=PACK)
                .unsqueeze(1)
                .to_broadcast([P, CHUNK_HEADS, PACK, HEAD_WORDS]),
                op=MULT,
            )
            crossed = products.tile([P, PACK, ROPE_WORDS], F32)
            result = crossed[:].rearrange("q t (h f j) -> q f h t j", h=CHUNK_HEADS, f=2)
            source = rotated.rearrange("q (h f j t) -> q f h t j", h=CHUNK_HEADS, f=2, t=PACK)
            sines = table[:, ROPE : 2 * ROPE].rearrange("q (f j t) -> q f t j", f=2, t=PACK)
            nc.vector.tensor_tensor(
                out=result[:, 1, :, :, 0:VECTOR_WORDS],
                in0=source[:, 0, :, :, 0:VECTOR_WORDS],
                in1=bank[:, ROPE:VECTOR_TABLE]
                .rearrange("q (j t) -> q t j", t=PACK)
                .unsqueeze(1)
                .to_broadcast([P, CHUNK_HEADS, PACK, VECTOR_WORDS]),
                op=MULT,
            )
            nc.gpsimd.tensor_tensor(
                out=result[:, 0],
                in0=source[:, 1],
                in1=sines[:, 1].unsqueeze(1).to_broadcast([P, CHUNK_HEADS, PACK, HALF_WORDS]),
                op=MULT,
            )
            nc.gpsimd.tensor_tensor(
                out=result[:, 1, :, :, VECTOR_WORDS:HALF_WORDS],
                in0=source[:, 0, :, :, VECTOR_WORDS:HALF_WORDS],
                in1=sines[:, 0, :, VECTOR_WORDS:HALF_WORDS]
                .unsqueeze(1)
                .to_broadcast([P, CHUNK_HEADS, PACK, HALF_WORDS - VECTOR_WORDS]),
                op=MULT,
            )
            return direct, crossed

        def sort_unrotated(k):
            if SORT_FROM <= k < TOKEN_CHUNKS:
                in_order = sorted_words.tile([P, CHUNK_NOPE // 2], F32)
                nc.scalar.copy(
                    out=in_order[:].rearrange("q (c u p) -> q c u p", c=NOPE_PASSES, u=2),
                    in_=words_of_passes(g_raws[k])[:, 0:NOPE_PASSES],
                )
                g_sorted[k] = in_order

        def unrotated_words(k):
            if k in g_sorted:
                return g_sorted[k][:].rearrange("q (c u p) -> q c u p", c=NOPE_PASSES, u=2)
            return words_of_passes(g_raws[k])

        def turn_pair(first_pass, g_raw, direct, crossed, g_grouped):
            if first_pass < NOPE_PASSES:
                nc.scalar.copy(
                    out=g_grouped[:, first_pass * K_PASS : (first_pass + 2) * K_PASS]
                    .bitcast(F32)
                    .rearrange("p (c r u) -> p c r u", c=2, u=2),
                    in_=turn_words(g_raw, first_pass),
                )
                return
            pair = range(first_pass, first_pass + 2)
            blocks = [slice((c - NOPE_PASSES) * P, (c - NOPE_PASSES + 1) * P) for c in pair]
            turned_a = turned_banks.tile([P, PACK, P], F32, tag="turned")
            turned_b = turned_banks.tile([P, PACK, P], F32, tag="turned")
            banks = [turned_a, turned_b]
            for t in range(PACK):
                for turned, block in zip(banks, blocks):
                    nc.tensor.matmul(
                        out=turned[:, t, :],
                        lhsT=direct[:, t, block],
                        rhs=ident[:],
                        is_transpose=True,
                        start=True,
                        stop=False,
                    )
                for turned, block in zip(banks, blocks):
                    nc.tensor.matmul(
                        out=turned[:, t, :],
                        lhsT=crossed[:, t, block],
                        rhs=ident[:],
                        is_transpose=True,
                        start=False,
                        stop=True,
                    )
            for turned, c in zip(banks, pair):
                nc.scalar.copy(
                    out=g_grouped[:, c * K_PASS : (c + 1) * K_PASS].rearrange(
                        "p (r t) -> p r t", t=PACK
                    ),
                    in_=turned[:].rearrange("p t r -> p r t"),
                )

        def quantise_tokens(g_grouped):
            g_codes = quantised.tile([P, CHUNK_PASSES * P], U32, align_bytes=64)
            g_scales = quantised.tile([P, CHUNK_PASSES * P], U8, align_bytes=64)
            nc.vector.quantize_mx(
                out=g_codes[:].bitcast(E5M2_X4), scales=g_scales[:], in_=g_grouped[:]
            )
            latest["codes"] = g_codes[:, 0:1]
            return g_codes, g_scales

        def multiply_passes(k, first_pass, g_codes, g_scales, sums):
            half = k % CHUNKS_IN_K
            for c in range(first_pass, first_pass + RUN):
                w_cols = slice(
                    (half * CHUNK_PASSES + c) * HIDDEN, (half * CHUNK_PASSES + c + 1) * HIDDEN
                )
                nc.tensor.matmul_mx(
                    out=sums[:],
                    lhsT=g_codes[:, c * P : (c + 1) * P].bitcast(E5M2_X4),
                    lhsT_scale=g_scales[:, c * P : (c + 1) * P],
                    rhs=w_codes[:, w_cols].bitcast(E4M3_X4),
                    rhs_scale=w_scales[:, w_cols],
                    start=(half == 0 and c == 0),
                    stop=(half == CHUNKS_IN_K - 1 and c == CHUNK_PASSES - 1),
                )

        def store_sums(n, sums):
            result = results.tile([P, HIDDEN], F32)
            nc.scalar.copy(out=result[:], in_=sums[:])
            nc.sync.dma_start(out=out[0, n * P : (n + 1) * P, :], in_=result[:])

        def fetch(k):
            if k < TOKEN_CHUNKS:
                if k == 0:
                    g_tables[0] = load_tables(0)
                g_raws[k] = load_tokens(k)
                n = k // CHUNKS_IN_K + 1
                if k % CHUNKS_IN_K == 0 and n < TOKEN_TILES:
                    g_tables[n] = load_tables(n)

        def multiply_by_tables(k):
            if k < TOKEN_CHUNKS:
                n = k // CHUNKS_IN_K
                if "codes" in latest:
                    nc.gpsimd.tensor_copy(out=gate_word[:], in_=latest["codes"])
                g_products[k] = rope_products(g_raws[k], g_tables[n], g_banks[n])

        def step(j):
            multiply_by_tables(j + 1)
            if 1 <= j <= TOKEN_CHUNKS:
                g_quantised[j - 1] = quantise_tokens(g_groupeds[j - 1])
            k = j - MX_LAG
            if j < TOKEN_CHUNKS:
                g_grouped = regrouped.tile([P, CHUNK], BF16, align_bytes=64, tag="grouped")
                g_groupeds[j] = g_grouped
            if k >= 0 and k % CHUNKS_IN_K == 0:
                sums = sum_banks.tile([P, HIDDEN], F32)
                g_sums[k // CHUNKS_IN_K] = sums
            next_tile = (j + 3) // CHUNKS_IN_K
            new_tables = j % CHUNKS_IN_K == 1 and next_tile < TOKEN_TILES
            if new_tables:
                sign_tables(next_tile)
            for first_pass in range(0, CHUNK_PASSES, RUN):
                if j < TOKEN_CHUNKS:
                    for c0 in range(first_pass, first_pass + RUN, 2):
                        if j < WARM_STEPS and c0 >= NOPE_PASSES:
                            keep_warm(2 if c0 == NOPE_PASSES else 1)
                        turn_pair(
                            c0, unrotated_words(j), g_products[j][0], g_products[j][1], g_groupeds[j]
                        )
                    sort_unrotated(j + 1)
                if k >= 0:
                    multiply_passes(
                        k, first_pass, g_quantised[k][0], g_quantised[k][1], g_sums[k // CHUNKS_IN_K]
                    )
                if first_pass == 0 and new_tables:
                    copy_tables(next_tile)
            if k >= 0 and k % CHUNKS_IN_K == CHUNKS_IN_K - 1:
                store_sums(k // CHUNKS_IN_K, g_sums[k // CHUNKS_IN_K])

        w_raws = {}
        fetch(0)
        w_raws[0] = load_weights(0)
        w_raws[1] = load_weights(1)
        fetch(1)
        w_raws[2] = load_weights(2)
        w_raws[3] = load_weights(3)
        fetch(2)
        w_raws[4] = load_weights(4)
        sign_tables(0)
        copy_tables(0)
        multiply_by_tables(0)
        quantise_weights(0, w_raws[0])
        sign_tables(1)
        quantise_weights(1, w_raws[1])
        copy_tables(1)
        w_raws[5] = load_weights(5)
        fetch(3)
        step(0)
        w_raws[6] = load_weights(6)
        quantise_weights(2, w_raws[2])
        quantise_weights(3, w_raws[3])
        w_raws[7] = load_weights(7)
        fetch(4)
        step(1)
        for j in range(2, TOKEN_CHUNKS + MX_LAG):
            for w in range(2 * j, min(2 * j + 2, WEIGHT_CHUNKS)):
                quantise_weights(w, w_raws[w])
            fetch(j + LOAD_AHEAD)
            step(j)
